import numpy as np
import ml_dtypes


def mxq(x, axis, fmt="e4m3"):
    dtype, down = {"e4m3": (ml_dtypes.float8_e4m3fn, 7), "e5m2": (ml_dtypes.float8_e5m2, 14)}[fmt]
    v = np.moveaxis(np.asarray(x, np.float32).astype(ml_dtypes.bfloat16).astype(np.float64), axis, -1)
    blocks = v.reshape(v.shape[:-1] + (-1, 32))
    amax = np.abs(blocks).max(-1, keepdims=True)
    byte = np.maximum(np.where(amax > 0, np.frexp(amax)[1] - 1 + 127, 0) - down, 1)
    scale = np.exp2(byte - 127.0)
    codes = (blocks / scale).astype(np.float32).astype(dtype).astype(np.float64)
    return np.moveaxis((codes * scale).reshape(v.shape), -1, axis)


WIDE = False


def mx_kscale(k):
    if not WIDE:
        return np.ones(k)
    levels = np.array([10, -10, 5, -5, 0])
    a = np.random.permutation(np.resize(levels, k // 512 * 4)).reshape(k // 512, 4)
    idx = np.arange(k)
    return np.exp2(a[idx // 512, idx % 128 // 32])


BF16 = ml_dtypes.bfloat16


def bf(x):
    return np.asarray(x, np.float32).astype(BF16)


def f64(x):
    return np.asarray(x).astype(np.float64)


N, E, C = 2048, 1024, 512
DENSITY = 0.01


def setup_inputs():
    s, t = mx_kscale(N), mx_kscale(C)
    member = np.random.uniform(size=(N, E)) < DENSITY
    return {"node_features": bf(np.random.standard_normal((N, C)) / s[:, None] * t[None, :]),
            "incidence": bf(member * s[:, None]),
            "W1": bf(np.random.standard_normal((C, C)) * np.sqrt(E) / np.sqrt(DENSITY * N * C) / t[:, None]),
            "b1": bf(np.random.standard_normal(C) * 0.1 * np.sqrt(E)),
            "edge_attention": bf(1.0 + np.random.standard_normal(E))}


def reference(node_features, incidence, W1, b1, edge_attention):
    agg = mxq(f64(incidence), 0, "e4m3").T @ mxq(f64(node_features), 0, "e4m3")
    lin = (mxq(agg, 1, "e4m3") @ mxq(f64(W1), 0, "e4m3")) + f64(b1)
    a = f64(edge_attention)
    e = np.exp(a - a.max())
    attn = e / e.sum()
    return lin * attn[:, None]

@@ -1,0 +1,317 @@
+import concourse.mybir as mybir
+from concourse.masks import make_identity
+
+BF16 = mybir.dt.bfloat16
+F32 = mybir.dt.float32
+U32 = mybir.dt.uint32
+U8 = mybir.dt.uint8
+FP8X4 = mybir.dt.float8_e4m3fn_x4
+ALU = mybir.AluOpType
+ACT = mybir.ActivationFunctionType
+AXIS = mybir.AxisListType
+
+N_NODES, N_EDGES, N_CH = 2048, 1024, 512
+
+P = 128
+PACK = 4
+K_PASS = P * PACK
+NODE_PASSES = N_NODES // K_PASS
+CH_TILES = N_CH // P
+EDGE_TILES = N_EDGES // P
+LOAD_EDGES = 512
+STEP_EDGES = 256
+STEPS = N_EDGES // STEP_EDGES
+STEP_TILES = STEP_EDGES // P
+LOADS = N_EDGES // LOAD_EDGES
+LOAD_STEPS = LOAD_EDGES // STEP_EDGES
+HALF = LOAD_EDGES // P
+RUN = 4
+
+FLOPS = 2 * N_EDGES * N_NODES * N_CH + 2 * N_EDGES * N_CH * N_CH
+
+assert CH_TILES == PACK
+assert NODE_PASSES * STEP_EDGES * PACK == 4096
+
+
+def regroup(copy, grouped, rows):
+    copy(
+        out=grouped.rearrange("p (c i) j -> p c j i", i=RUN),
+        in_=rows.rearrange("p j (c i) -> p c j i", i=RUN),
+    )
+
+
+def tile_heterogeneoustemporalhypergraphnn_pa_kernel(
+    tc, node_features, incidence, W1, b1, edge_attention, out
+):
+    nc = tc.nc
+
+    def regrouping_copy(c, s):
+        return nc.scalar.copy if (c + s) % 2 == 0 else nc.vector.tensor_copy
+
+    with tc.tile_pool(name="rows", bufs=1) as rows_pool, tc.tile_pool(
+        name="grouped", bufs=1
+    ) as grouped_pool, tc.tile_pool(name="mx", bufs=1) as mx_pool, tc.tile_pool(
+        name="small", bufs=1
+    ) as small_pool, tc.tile_pool(name="result", bufs=4) as result_pool, tc.manual_schedule():
+
+        logit_rows = small_pool.tile([P, P], BF16)
+        bias_rows = small_pool.tile([P, N_CH], BF16)
+        ones_bf = small_pool.tile([P, P], BF16)
+        ones_f32 = small_pool.tile([P, P], F32)
+        ident_bf = small_pool.tile([P, P], BF16)
+        table_warm = small_pool.tile([P, 1], F32)
+        nc.gpsimd.memset(logit_rows[:], 0.0)
+        nc.gpsimd.memset(bias_rows[:], 0.0)
+        nc.vector.memset(table_warm[:], 0.0)
+        nc.vector.memset(ones_bf[:], 1.0)
+        nc.vector.memset(ones_f32[:], 1.0)
+        make_identity(nc, ident_bf[:])
+        nc.scalar.activation(out=table_warm[:], in_=table_warm[:], func=ACT.Exp)
+
+        nc.sync.dma_start(
+            out=logit_rows[0:EDGE_TILES, :],
+            in_=edge_attention.rearrange("(i q) -> i q", q=P),
+        )
+        nf_rows = []
+        for c in range(NODE_PASSES):
+            piece = rows_pool.tile([P, PACK, N_CH], BF16, name="nf_rows%d" % c)
+            nc.sync.dma_start(
+                out=piece[:],
+                in_=node_features[c * K_PASS : (c + 1) * K_PASS, :].rearrange(
+                    "(p j) w -> p j w", j=PACK
+                ),
+            )
+            nf_rows.append(piece)
+        nc.sync.dma_start(out=bias_rows[0:1, :], in_=b1.rearrange("(o n) -> o n", o=1))
+        inc_rows = []
+        for h in range(LOADS):
+            pieces = []
+            for c in range(NODE_PASSES):
+                piece = rows_pool.tile([P, PACK, LOAD_EDGES], BF16, name="inc_rows%d_%d" % (h, c))
+                nc.sync.dma_start(
+                    out=piece[:],
+                    in_=incidence[
+                        c * K_PASS : (c + 1) * K_PASS,
+                        h * LOAD_EDGES : (h + 1) * LOAD_EDGES,
+                    ].rearrange("(p j) w -> p j w", j=PACK),
+                )
+                pieces.append(piece)
+            inc_rows.append(pieces)
+        w1_rows = rows_pool.tile([P, PACK, N_CH], BF16)
+        nc.sync.dma_start(out=w1_rows[:], in_=W1.rearrange("(t p) n -> p t n", p=P))
+
+        logit_col = small_pool.tile([P, EDGE_TILES], F32)
+        part_max = small_pool.tile([P, 1], F32)
+        part_max_bf = small_pool.tile([P, 1], BF16)
+        all_max = small_pool.tile([P, 1], F32)
+        shifted = small_pool.tile([P, EDGE_TILES], F32)
+        exp_col = small_pool.tile([P, EDGE_TILES], F32)
+        exp_sum = small_pool.tile([P, 1], F32)
+        inv_sum = small_pool.tile([P, 1], F32)
+        attn_col = small_pool.tile([P, EDGE_TILES], F32)
+
+        def softmax_partial_max():
+            nc.tensor.transpose(logit_ps[:], logit_rows[:], ident_bf[:])
+            nc.vector.tensor_copy(out=logit_col[:], in_=logit_ps[:, 0:EDGE_TILES])
+            nc.vector.tensor_reduce(out=part_max[:], in_=logit_col[:], axis=AXIS.X, op=ALU.max)
+            nc.vector.tensor_copy(out=part_max_bf[:], in_=part_max[:])
+            nc.tensor.matmul(
+                out=max_ps[:],
+                lhsT=part_max_bf[:, 0:1].to_broadcast([P, P]),
+                rhs=ident_bf[:],
+                start=True,
+                stop=True,
+            )
+
+        def softmax_exp():
+            nc.vector.tensor_reduce(out=all_max[:], in_=max_ps[:], axis=AXIS.X, op=ALU.max)
+            nc.vector.tensor_scalar(
+                out=shifted[:],
+                in0=logit_col[:],
+                scalar1=all_max[:, 0:1],
+                scalar2=None,
+                op0=ALU.subtract,
+            )
+            nc.scalar.activation(out=exp_col[:], in_=shifted[:], func=ACT.Exp)
+            nc.tensor.matmul(out=sum_ps[:], lhsT=ones_f32[:], rhs=exp_col[:], start=True, stop=True)
+
+        def softmax_normalise():
+            nc.vector.tensor_reduce(out=exp_sum[:], in_=sum_ps[:], axis=AXIS.X, op=ALU.add)
+            nc.vector.reciprocal(out=inv_sum[:], in_=exp_sum[:])
+            nc.vector.tensor_scalar(
+                out=attn_col[:],
+                in0=exp_col[:],
+                scalar1=inv_sum[:, 0:1],
+                scalar2=None,
+                op0=ALU.mult,
+            )
+
+        bias_all = small_pool.tile([P, N_CH], F32)
+        bias_attn = small_pool.tile([P, EDGE_TILES, N_CH], F32)
+
+        def spread_bias():
+            nc.tensor.matmul(out=bias_ps[:], lhsT=ones_bf[:], rhs=bias_rows[:], start=True, stop=True)
+            nc.scalar.copy(out=bias_all[:], in_=bias_ps[:])
+
+        def scale_bias(i):
+            nc.vector.tensor_scalar(
+                out=bias_attn[:, i, :],
+                in0=bias_all[:],
+                scalar1=attn_col[:, i : i + 1],
+                scalar2=None,
+                op0=ALU.mult,
+            )
+
+        nf_grouped = grouped_pool.tile([P, NODE_PASSES, N_CH, PACK], BF16, align_bytes=64)
+        nf_codes = mx_pool.tile([P, NODE_PASSES, N_CH], U32, align_bytes=64)
+        nf_scales = mx_pool.tile([P, NODE_PASSES, N_CH], U8, align_bytes=64)
+
+        def regroup_nf(c):
+            regroup(regrouping_copy(c, 0), nf_grouped[:, c], nf_rows[c][:])
+
+        def quantise_nf(c):
+            nc.vector.quantize_mx(
+                out=nf_codes[:, c, :].bitcast(FP8X4),
+                scales=nf_scales[:, c, :],
+                in_=nf_grouped[:, c].rearrange("p w j -> p (w j)"),
+            )
+
+        with tc.psum_pool(name="setup_psum", bufs=1) as setup_psum:
+            logit_ps = setup_psum.tile([P, P], BF16)
+            max_ps = setup_psum.tile([P, P], F32)
+            sum_ps = setup_psum.tile([P, EDGE_TILES], F32)
+            bias_ps = setup_psum.tile([P, N_CH], F32)
+            regroup_nf(0)
+            regroup_nf(1)
+            softmax_partial_max()
+            quantise_nf(0)
+            softmax_exp()
+            quantise_nf(1)
+            regroup_nf(2)
+            regroup_nf(3)
+            spread_bias()
+            softmax_normalise()
+            quantise_nf(2)
+            quantise_nf(3)
+
+        inc_grouped = []
+        inc_codes = []
+        inc_scales = []
+        for s in range(STEPS):
+            inc_grouped.append(
+                grouped_pool.tile(
+                    [P, NODE_PASSES, STEP_EDGES, PACK], BF16, align_bytes=64, name="inc_grouped%d" % s
+                )
+            )
+            inc_codes.append(
+                mx_pool.tile([P, NODE_PASSES, STEP_EDGES], U32, align_bytes=64, name="inc_codes%d" % s)
+            )
+            inc_scales.append(
+                mx_pool.tile([P, NODE_PASSES, STEP_EDGES], U8, align_bytes=64, name="inc_scales%d" % s)
+            )
+
+        def regroup_incidence(h, c):
+            for k in range(LOAD_STEPS):
+                s = h * LOAD_STEPS + k
+                cols = slice(k * STEP_EDGES, (k + 1) * STEP_EDGES)
+                regroup(regrouping_copy(c, s), inc_grouped[s][:, c], inc_rows[h][c][:, :, cols])
+
+        def quantise_incidence(s):
+            nc.vector.quantize_mx(
+                out=inc_codes[s][:].rearrange("p c w -> p (c w)").bitcast(FP8X4),
+                scales=inc_scales[s][:].rearrange("p c w -> p (c w)"),
+                in_=inc_grouped[s][:].rearrange("p c w j -> p (c w j)"),
+            )
+
+        w1_grouped = grouped_pool.tile([P, N_CH, PACK], BF16, align_bytes=64)
+        w1_codes = mx_pool.tile([P, N_CH], U32, align_bytes=64)
+        w1_scales = mx_pool.tile([P, N_CH], U8, align_bytes=64)
+
+        agg_grouped = grouped_pool.tile([P, EDGE_TILES, P, PACK], BF16, align_bytes=64)
+        agg_codes = mx_pool.tile([P, EDGE_TILES, P], U32, align_bytes=64)
+        agg_scales = mx_pool.tile([P, EDGE_TILES, P], U8, align_bytes=64)
+        agg_banks = {}
+        lin_banks = {}
+
+        def aggregate(i):
+            s = i // STEP_TILES
+            edges = slice((i % STEP_TILES) * P, (i % STEP_TILES + 1) * P)
+            agg_banks[i] = main_psum.tile([P, CH_TILES, P], F32, tag="agg", name="agg_ps%d" % i)
+            for t in range(CH_TILES):
+                channels = slice(t * P, (t + 1) * P)
+                for c in range(NODE_PASSES):
+                    nc.tensor.matmul_mx(
+                        out=agg_banks[i][:, t, :],
+                        lhsT=nf_codes[:, c, channels].bitcast(FP8X4),
+                        lhsT_scale=nf_scales[:, c, channels],
+                        rhs=inc_codes[s][:, c, edges].bitcast(FP8X4),
+                        rhs_scale=inc_scales[s][:, c, edges],
+                        start=(c == 0),
+                        stop=(c == NODE_PASSES - 1),
+                    )
+
+        def round_agg(i):
+            nc.scalar.copy(out=agg_grouped[:, i], in_=agg_banks[i][:].rearrange("p t e -> p e t"))
+
+        def project(i):
+            nc.vector.quantize_mx(
+                out=agg_codes[:, i, :].bitcast(FP8X4),
+                scales=agg_scales[:, i, :],
+                in_=agg_grouped[:, i].rearrange("p e t -> p (e t)"),
+            )
+            lin_banks[i] = main_psum.tile([P, N_CH], F32, tag="lin", name="lin_ps%d" % i)
+            nc.tensor.matmul_mx(
+                out=lin_banks[i][:],
+                lhsT=agg_codes[:, i, :].bitcast(FP8X4),
+                lhsT_scale=agg_scales[:, i, :],
+                rhs=w1_codes[:].bitcast(FP8X4),
+                rhs_scale=w1_scales[:],
+                start=True,
+                stop=True,
+            )
+
+        def finish(i):
+            result = result_pool.tile([P, N_CH], F32)
+            nc.vector.scalar_tensor_tensor(
+                out=result[:],
+                in0=lin_banks[i][:],
+                scalar=attn_col[:, i : i + 1],
+                in1=bias_attn[:, i, :],
+                op0=ALU.mult,
+                op1=ALU.add,
+            )
+            nc.sync.dma_start(out=out[i * P : (i + 1) * P, :], in_=result[:])
+
+        with tc.psum_pool(name="main_psum", bufs=HALF) as main_psum:
+            for c in range(NODE_PASSES):
+                regroup_incidence(0, c)
+                scale_bias(2 * c)
+                scale_bias(2 * c + 1)
+            for s in range(LOAD_STEPS):
+                quantise_incidence(s)
+                for i in range(s * STEP_TILES, (s + 1) * STEP_TILES):
+                    aggregate(i)
+            for c in range(NODE_PASSES):
+                regroup_incidence(1, c)
+            regroup(nc.scalar.copy, w1_grouped[:], w1_rows[:])
+            for i in range(HALF):
+                round_agg(i)
+            quantise_incidence(LOAD_STEPS)
+            aggregate(HALF)
+            aggregate(HALF + 1)
+            quantise_incidence(LOAD_STEPS + 1)
+            nc.vector.quantize_mx(
+                out=w1_codes[:].bitcast(FP8X4),
+                scales=w1_scales[:],
+                in_=w1_grouped[:].rearrange("p n t -> p (n t)"),
+            )
+            for i in range(HALF):
+                project(i)
+            aggregate(HALF + 2)
+            aggregate(HALF + 3)
+            for i in range(HALF):
+                finish(i)
+                round_agg(HALF + i)
+                project(HALF + i)
+            for i in range(HALF, EDGE_TILES):
+                finish(i)

@@ -154,12 +154,13 @@ def tile_heterogeneoustemporalhypergraphnn_pa_kernel(
             nc.scalar.copy(out=bias_all[:], in_=bias_ps[:])
 
         def scale_bias(i):
-            nc.vector.tensor_scalar(
+            nc.gpsimd.tensor_scalar(
                 out=bias_attn[:, i, :],
                 in0=bias_all[:],
                 scalar1=attn_col[:, i : i + 1],
-                scalar2=None,
+                scalar2=0.0,
                 op0=ALU.mult,
+                op1=ALU.add,
             )
 
         nf_grouped = grouped_pool.tile([P, NODE_PASSES, N_CH, PACK], BF16, align_bytes=64)
@@ -283,10 +284,10 @@ def tile_heterogeneoustemporalhypergraphnn_pa_kernel(
             nc.sync.dma_start(out=out[i * P : (i + 1) * P, :], in_=result[:])
 
         with tc.psum_pool(name="main_psum", bufs=HALF) as main_psum:
+            for i in range(EDGE_TILES):
+                scale_bias(i)
             for c in range(NODE_PASSES):
                 regroup_incidence(0, c)
-                scale_bias(2 * c)
-                scale_bias(2 * c + 1)
             for s in range(LOAD_STEPS):
                 quantise_incidence(s)
                 for i in range(s * STEP_TILES, (s + 1) * STEP_TILES):

@@ -15,29 +15,18 @@ N_NODES, N_EDGES, N_CH = 2048, 1024, 512
 P = 128
 PACK = 4
 K_PASS = P * PACK
+WIDTH = 512
 NODE_PASSES = N_NODES // K_PASS
 CH_TILES = N_CH // P
 EDGE_TILES = N_EDGES // P
-LOAD_EDGES = 512
-STEP_EDGES = 256
-STEPS = N_EDGES // STEP_EDGES
-STEP_TILES = STEP_EDGES // P
-LOADS = N_EDGES // LOAD_EDGES
-LOAD_STEPS = LOAD_EDGES // STEP_EDGES
-HALF = LOAD_EDGES // P
+HALVES = N_EDGES // WIDTH
+HALF = WIDTH // P
 RUN = 4
+SCALAR_COLS = 256
 
 FLOPS = 2 * N_EDGES * N_NODES * N_CH + 2 * N_EDGES * N_CH * N_CH
 
-assert CH_TILES == PACK
-assert NODE_PASSES * STEP_EDGES * PACK == 4096
-
-
-def regroup(copy, grouped, rows):
-    copy(
-        out=grouped.rearrange("p (c i) j -> p c j i", i=RUN),
-        in_=rows.rearrange("p j (c i) -> p c j i", i=RUN),
-    )
+assert CH_TILES == PACK and N_CH == WIDTH
 
 
 def tile_heterogeneoustemporalhypergraphnn_pa_kernel(
@@ -45,14 +34,40 @@ def tile_heterogeneoustemporalhypergraphnn_pa_kernel(
 ):
     nc = tc.nc
 
-    def regrouping_copy(c, s):
-        return nc.scalar.copy if (c + s) % 2 == 0 else nc.vector.tensor_copy
+    with tc.tile_pool(name="chunks", bufs=1) as chunk_pool, tc.tile_pool(
+        name="agg", bufs=1
+    ) as agg_pool, tc.tile_pool(name="small", bufs=1) as small_pool, tc.tile_pool(
+        name="result", bufs=4
+    ) as result_pool:
 
-    with tc.tile_pool(name="rows", bufs=1) as rows_pool, tc.tile_pool(
-        name="grouped", bufs=1
-    ) as grouped_pool, tc.tile_pool(name="mx", bufs=1) as mx_pool, tc.tile_pool(
-        name="small", bufs=1
-    ) as small_pool, tc.tile_pool(name="result", bufs=4) as result_pool, tc.manual_schedule():
+        def load_chunk(name, rows_of_partition):
+            chunk = {
+                "rows": chunk_pool.tile([P, PACK, WIDTH], BF16, name=name + "_rows"),
+                "grouped": chunk_pool.tile(
+                    [P, WIDTH, PACK], BF16, align_bytes=64, name=name + "_grouped"
+                ),
+                "codes": chunk_pool.tile([P, WIDTH], U32, align_bytes=64, name=name + "_codes"),
+                "scales": chunk_pool.tile([P, WIDTH], U8, align_bytes=64, name=name + "_scales"),
+            }
+            nc.sync.dma_start(out=chunk["rows"][:], in_=rows_of_partition)
+            return chunk
+
+        def regroup_columns(copy, chunk, cols):
+            copy(
+                out=chunk["grouped"][:, cols, :].rearrange("p (c i) j -> p c j i", i=RUN),
+                in_=chunk["rows"][:, :, cols].rearrange("p j (c i) -> p c j i", i=RUN),
+            )
+
+        def regroup(chunk):
+            regroup_columns(nc.scalar.copy, chunk, slice(0, SCALAR_COLS))
+            regroup_columns(nc.vector.tensor_copy, chunk, slice(SCALAR_COLS, WIDTH))
+
+        def quantise(chunk):
+            nc.vector.quantize_mx(
+                out=chunk["codes"][:].bitcast(FP8X4),
+                scales=chunk["scales"][:],
+                in_=chunk["grouped"][:].rearrange("p w j -> p (w j)"),
+            )
 
         logit_rows = small_pool.tile([P, P], BF16)
         bias_rows = small_pool.tile([P, N_CH], BF16)
@@ -72,33 +87,27 @@ def tile_heterogeneoustemporalhypergraphnn_pa_kernel(
             out=logit_rows[0:EDGE_TILES, :],
             in_=edge_attention.rearrange("(i q) -> i q", q=P),
         )
-        nf_rows = []
-        for c in range(NODE_PASSES):
-            piece = rows_pool.tile([P, PACK, N_CH], BF16, name="nf_rows%d" % c)
-            nc.sync.dma_start(
-                out=piece[:],
-                in_=node_features[c * K_PASS : (c + 1) * K_PASS, :].rearrange(
-                    "(p j) w -> p j w", j=PACK
-                ),
+        nf = [
+            load_chunk(
+                "nf%d" % c,
+                node_features[c * K_PASS : (c + 1) * K_PASS, :].rearrange("(p j) w -> p j w", j=PACK),
             )
-            nf_rows.append(piece)
+            for c in range(NODE_PASSES)
+        ]
         nc.sync.dma_start(out=bias_rows[0:1, :], in_=b1.rearrange("(o n) -> o n", o=1))
-        inc_rows = []
-        for h in range(LOADS):
-            pieces = []
-            for c in range(NODE_PASSES):
-                piece = rows_pool.tile([P, PACK, LOAD_EDGES], BF16, name="inc_rows%d_%d" % (h, c))
-                nc.sync.dma_start(
-                    out=piece[:],
-                    in_=incidence[
-                        c * K_PASS : (c + 1) * K_PASS,
-                        h * LOAD_EDGES : (h + 1) * LOAD_EDGES,
-                    ].rearrange("(p j) w -> p j w", j=PACK),
+        inc = [
+            [
+                load_chunk(
+                    "inc%d_%d" % (h, c),
+                    incidence[c * K_PASS : (c + 1) * K_PASS, h * WIDTH : (h + 1) * WIDTH].rearrange(
+                        "(p j) w -> p j w", j=PACK
+                    ),
                 )
-                pieces.append(piece)
-            inc_rows.append(pieces)
-        w1_rows = rows_pool.tile([P, PACK, N_CH], BF16)
-        nc.sync.dma_start(out=w1_rows[:], in_=W1.rearrange("(t p) n -> p t n", p=P))
+                for c in range(NODE_PASSES)
+            ]
+            for h in range(HALVES)
+        ]
+        w1 = load_chunk("w1", W1.rearrange("(t p) n -> p t n", p=P))
 
         logit_col = small_pool.tile([P, EDGE_TILES], F32)
         part_max = small_pool.tile([P, 1], F32)
@@ -163,90 +172,25 @@ def tile_heterogeneoustemporalhypergraphnn_pa_kernel(
                 op1=ALU.add,
             )
 
-        nf_grouped = grouped_pool.tile([P, NODE_PASSES, N_CH, PACK], BF16, align_bytes=64)
-        nf_codes = mx_pool.tile([P, NODE_PASSES, N_CH], U32, align_bytes=64)
-        nf_scales = mx_pool.tile([P, NODE_PASSES, N_CH], U8, align_bytes=64)
-
-        def regroup_nf(c):
-            regroup(regrouping_copy(c, 0), nf_grouped[:, c], nf_rows[c][:])
-
-        def quantise_nf(c):
-            nc.vector.quantize_mx(
-                out=nf_codes[:, c, :].bitcast(FP8X4),
-                scales=nf_scales[:, c, :],
-                in_=nf_grouped[:, c].rearrange("p w j -> p (w j)"),
-            )
-
-        with tc.psum_pool(name="setup_psum", bufs=1) as setup_psum:
-            logit_ps = setup_psum.tile([P, P], BF16)
-            max_ps = setup_psum.tile([P, P], F32)
-            sum_ps = setup_psum.tile([P, EDGE_TILES], F32)
-            bias_ps = setup_psum.tile([P, N_CH], F32)
-            regroup_nf(0)
-            regroup_nf(1)
-            softmax_partial_max()
-            quantise_nf(0)
-            softmax_exp()
-            quantise_nf(1)
-            regroup_nf(2)
-            regroup_nf(3)
-            spread_bias()
-            softmax_normalise()
-            quantise_nf(2)
-            quantise_nf(3)
-
-        inc_grouped = []
-        inc_codes = []
-        inc_scales = []
-        for s in range(STEPS):
-            inc_grouped.append(
-                grouped_pool.tile(
-                    [P, NODE_PASSES, STEP_EDGES, PACK], BF16, align_bytes=64, name="inc_grouped%d" % s
-                )
-            )
-            inc_codes.append(
-                mx_pool.tile([P, NODE_PASSES, STEP_EDGES], U32, align_bytes=64, name="inc_codes%d" % s)
-            )
-            inc_scales.append(
-                mx_pool.tile([P, NODE_PASSES, STEP_EDGES], U8, align_bytes=64, name="inc_scales%d" % s)
-            )
-
-        def regroup_incidence(h, c):
-            for k in range(LOAD_STEPS):
-                s = h * LOAD_STEPS + k
-                cols = slice(k * STEP_EDGES, (k + 1) * STEP_EDGES)
-                regroup(regrouping_copy(c, s), inc_grouped[s][:, c], inc_rows[h][c][:, :, cols])
-
-        def quantise_incidence(s):
-            nc.vector.quantize_mx(
-                out=inc_codes[s][:].rearrange("p c w -> p (c w)").bitcast(FP8X4),
-                scales=inc_scales[s][:].rearrange("p c w -> p (c w)"),
-                in_=inc_grouped[s][:].rearrange("p c w j -> p (c w j)"),
-            )
-
-        w1_grouped = grouped_pool.tile([P, N_CH, PACK], BF16, align_bytes=64)
-        w1_codes = mx_pool.tile([P, N_CH], U32, align_bytes=64)
-        w1_scales = mx_pool.tile([P, N_CH], U8, align_bytes=64)
-
-        agg_grouped = grouped_pool.tile([P, EDGE_TILES, P, PACK], BF16, align_bytes=64)
-        agg_codes = mx_pool.tile([P, EDGE_TILES, P], U32, align_bytes=64)
-        agg_scales = mx_pool.tile([P, EDGE_TILES, P], U8, align_bytes=64)
+        agg_grouped = agg_pool.tile([P, EDGE_TILES, P, PACK], BF16, align_bytes=64)
+        agg_codes = agg_pool.tile([P, EDGE_TILES, P], U32, align_bytes=64)
+        agg_scales = agg_pool.tile([P, EDGE_TILES, P], U8, align_bytes=64)
         agg_banks = {}
         lin_banks = {}
 
         def aggregate(i):
-            s = i // STEP_TILES
-            edges = slice((i % STEP_TILES) * P, (i % STEP_TILES + 1) * P)
+            half = inc[i // HALF]
+            edges = slice((i % HALF) * P, (i % HALF + 1) * P)
             agg_banks[i] = main_psum.tile([P, CH_TILES, P], F32, tag="agg", name="agg_ps%d" % i)
             for t in range(CH_TILES):
                 channels = slice(t * P, (t + 1) * P)
                 for c in range(NODE_PASSES):
                     nc.tensor.matmul_mx(
                         out=agg_banks[i][:, t, :],
-                        lhsT=nf_codes[:, c, channels].bitcast(FP8X4),
-                        lhsT_scale=nf_scales[:, c, channels],
-                        rhs=inc_codes[s][:, c, edges].bitcast(FP8X4),
-                        rhs_scale=inc_scales[s][:, c, edges],
+                        lhsT=nf[c]["codes"][:, channels].bitcast(FP8X4),
+                        lhsT_scale=nf[c]["scales"][:, channels],
+                        rhs=half[c]["codes"][:, edges].bitcast(FP8X4),
+                        rhs_scale=half[c]["scales"][:, edges],
                         start=(c == 0),
                         stop=(c == NODE_PASSES - 1),
                     )
@@ -254,19 +198,21 @@ def tile_heterogeneoustemporalhypergraphnn_pa_kernel(
         def round_agg(i):
             nc.scalar.copy(out=agg_grouped[:, i], in_=agg_banks[i][:].rearrange("p t e -> p e t"))
 
-        def project(i):
+        def quantise_agg(i):
             nc.vector.quantize_mx(
                 out=agg_codes[:, i, :].bitcast(FP8X4),
                 scales=agg_scales[:, i, :],
                 in_=agg_grouped[:, i].rearrange("p e t -> p (e t)"),
             )
+
+        def project(i):
             lin_banks[i] = main_psum.tile([P, N_CH], F32, tag="lin", name="lin_ps%d" % i)
             nc.tensor.matmul_mx(
                 out=lin_banks[i][:],
                 lhsT=agg_codes[:, i, :].bitcast(FP8X4),
                 lhsT_scale=agg_scales[:, i, :],
-                rhs=w1_codes[:].bitcast(FP8X4),
-                rhs_scale=w1_scales[:],
+                rhs=w1["codes"][:].bitcast(FP8X4),
+                rhs_scale=w1["scales"][:],
                 start=True,
                 stop=True,
             )
@@ -283,29 +229,46 @@ def tile_heterogeneoustemporalhypergraphnn_pa_kernel(
             )
             nc.sync.dma_start(out=out[i * P : (i + 1) * P, :], in_=result[:])
 
+        with tc.psum_pool(name="setup_psum", bufs=1) as setup_psum:
+            logit_ps = setup_psum.tile([P, P], BF16)
+            max_ps = setup_psum.tile([P, P], F32)
+            sum_ps = setup_psum.tile([P, EDGE_TILES], F32)
+            bias_ps = setup_psum.tile([P, N_CH], F32)
+            softmax_partial_max()
+            softmax_exp()
+            regroup(nf[0])
+            softmax_normalise()
+            for c in range(1, NODE_PASSES):
+                regroup(nf[c])
+                quantise(nf[c - 1])
+            spread_bias()
+        for i in range(EDGE_TILES):
+            scale_bias(i)
+
         with tc.psum_pool(name="main_psum", bufs=HALF) as main_psum:
-            for i in range(EDGE_TILES):
-                scale_bias(i)
-            for c in range(NODE_PASSES):
-                regroup_incidence(0, c)
-            for s in range(LOAD_STEPS):
-                quantise_incidence(s)
-                for i in range(s * STEP_TILES, (s + 1) * STEP_TILES):
-                    aggregate(i)
-            for c in range(NODE_PASSES):
-                regroup_incidence(1, c)
-            regroup(nc.scalar.copy, w1_grouped[:], w1_rows[:])
+            regroup(inc[0][0])
+            quantise(nf[3])
+            for c in range(1, NODE_PASSES):
+                regroup(inc[0][c])
+                quantise(inc[0][c - 1])
+            quantise(inc[0][NODE_PASSES - 1])
             for i in range(HALF):
+                aggregate(i)
+            regroup(inc[1][0])
+            for c in range(1, NODE_PASSES):
+                regroup(inc[1][c])
+                quantise(inc[1][c - 1])
+            quantise(inc[1][NODE_PASSES - 1])
+            for i in range(HALF // 2):
                 round_agg(i)
-            quantise_incidence(LOAD_STEPS)
-            aggregate(HALF)
-            aggregate(HALF + 1)
-            quantise_incidence(LOAD_STEPS + 1)
-            nc.vector.quantize_mx(
-                out=w1_codes[:].bitcast(FP8X4),
-                scales=w1_scales[:],
-                in_=w1_grouped[:].rearrange("p n t -> p (n t)"),
-            )
+                aggregate(HALF + i)
+            regroup(w1)
+            for i in range(HALF // 2):
+                quantise_agg(i)
+            quantise(w1)
+            for i in range(HALF // 2, HALF):
+                round_agg(i)
+                quantise_agg(i)
             for i in range(HALF):
                 project(i)
             aggregate(HALF + 2)
@@ -313,6 +276,7 @@ def tile_heterogeneoustemporalhypergraphnn_pa_kernel(
             for i in range(HALF):
                 finish(i)
                 round_agg(HALF + i)
+                quantise_agg(HALF + i)
                 project(HALF + i)
             for i in range(HALF, EDGE_TILES):
                 finish(i)

@@ -19,8 +19,8 @@ WIDTH = 512
 NODE_PASSES = N_NODES // K_PASS
 CH_TILES = N_CH // P
 EDGE_TILES = N_EDGES // P
-HALVES = N_EDGES // WIDTH
-HALF = WIDTH // P
+EDGE_CHUNKS = N_EDGES // WIDTH
+CHUNK_TILES = WIDTH // P
 RUN = 4
 SCALAR_COLS = 256
 
@@ -39,18 +39,20 @@ def tile_heterogeneoustemporalhypergraphnn_pa_kernel(
     ) as agg_pool, tc.tile_pool(name="small", bufs=1) as small_pool, tc.tile_pool(
         name="result", bufs=4
     ) as result_pool:
+        def load_rows(name, width, rows_of_partition):
+            rows = chunk_pool.tile([P, PACK, width], BF16, name=name + "_rows")
+            nc.sync.dma_start(out=rows[:], in_=rows_of_partition)
+            return rows
 
-        def load_chunk(name, rows_of_partition):
-            chunk = {
-                "rows": chunk_pool.tile([P, PACK, WIDTH], BF16, name=name + "_rows"),
+        def new_chunk(name, rows):
+            return {
+                "rows": rows,
                 "grouped": chunk_pool.tile(
                     [P, WIDTH, PACK], BF16, align_bytes=64, name=name + "_grouped"
                 ),
                 "codes": chunk_pool.tile([P, WIDTH], U32, align_bytes=64, name=name + "_codes"),
                 "scales": chunk_pool.tile([P, WIDTH], U8, align_bytes=64, name=name + "_scales"),
             }
-            nc.sync.dma_start(out=chunk["rows"][:], in_=rows_of_partition)
-            return chunk
 
         def regroup_columns(copy, chunk, cols):
             copy(
@@ -87,27 +89,28 @@ def tile_heterogeneoustemporalhypergraphnn_pa_kernel(
             out=logit_rows[0:EDGE_TILES, :],
             in_=edge_attention.rearrange("(i q) -> i q", q=P),
         )
-        nf = [
-            load_chunk(
-                "nf%d" % c,
-                node_features[c * K_PASS : (c + 1) * K_PASS, :].rearrange("(p j) w -> p j w", j=PACK),
+        nf = []
+        inc = []
+        for c in range(NODE_PASSES):
+            nodes = slice(c * K_PASS, (c + 1) * K_PASS)
+            nf_rows = load_rows(
+                "nf%d" % c, N_CH, node_features[nodes, :].rearrange("(p j) w -> p j w", j=PACK)
             )
-            for c in range(NODE_PASSES)
-        ]
-        nc.sync.dma_start(out=bias_rows[0:1, :], in_=b1.rearrange("(o n) -> o n", o=1))
-        inc = [
-            [
-                load_chunk(
-                    "inc%d_%d" % (h, c),
-                    incidence[c * K_PASS : (c + 1) * K_PASS, h * WIDTH : (h + 1) * WIDTH].rearrange(
-                        "(p j) w -> p j w", j=PACK
-                    ),
-                )
-                for c in range(NODE_PASSES)
-            ]
-            for h in range(HALVES)
-        ]
-        w1 = load_chunk("w1", W1.rearrange("(t p) n -> p t n", p=P))
+            if c == 0:
+                nc.sync.dma_start(out=bias_rows[0:1, :], in_=b1.rearrange("(o n) -> o n", o=1))
+            if c == NODE_PASSES - 1:
+                w1_rows = load_rows("w1", N_CH, W1.rearrange("(t p) n -> p t n", p=P))
+            inc_rows = load_rows(
+                "inc%d" % c, N_EDGES, incidence[nodes, :].rearrange("(p j) w -> p j w", j=PACK)
+            )
+            nf.append(new_chunk("nf%d" % c, nf_rows[:]))
+            inc.append(
+                [
+                    new_chunk("inc%d_%d" % (c, h), inc_rows[:, :, h * WIDTH : (h + 1) * WIDTH])
+                    for h in range(EDGE_CHUNKS)
+                ]
+            )
+        w1 = new_chunk("w1", w1_rows[:])
 
         logit_col = small_pool.tile([P, EDGE_TILES], F32)
         part_max = small_pool.tile([P, 1], F32)
@@ -175,24 +178,22 @@ def tile_heterogeneoustemporalhypergraphnn_pa_kernel(
         agg_grouped = agg_pool.tile([P, EDGE_TILES, P, PACK], BF16, align_bytes=64)
         agg_codes = agg_pool.tile([P, EDGE_TILES, P], U32, align_bytes=64)
         agg_scales = agg_pool.tile([P, EDGE_TILES, P], U8, align_bytes=64)
-        agg_banks = {}
+        agg_banks = []
         lin_banks = {}
 
-        def aggregate(i):
-            half = inc[i // HALF]
-            edges = slice((i % HALF) * P, (i % HALF + 1) * P)
-            agg_banks[i] = main_psum.tile([P, CH_TILES, P], F32, tag="agg", name="agg_ps%d" % i)
-            for t in range(CH_TILES):
-                channels = slice(t * P, (t + 1) * P)
-                for c in range(NODE_PASSES):
+        def accumulate(c, h):
+            for k in range(CHUNK_TILES):
+                edges = slice(k * P, (k + 1) * P)
+                for t in range(CH_TILES):
+                    channels = slice(t * P, (t + 1) * P)
                     nc.tensor.matmul_mx(
-                        out=agg_banks[i][:, t, :],
+                        out=agg_banks[h * CHUNK_TILES + k][:, t, :],
                         lhsT=nf[c]["codes"][:, channels].bitcast(FP8X4),
                         lhsT_scale=nf[c]["scales"][:, channels],
-                        rhs=half[c]["codes"][:, edges].bitcast(FP8X4),
-                        rhs_scale=half[c]["scales"][:, edges],
-                        start=(c == 0),
-                        stop=(c == NODE_PASSES - 1),
+                        rhs=inc[c][h]["codes"][:, edges].bitcast(FP8X4),
+                        rhs_scale=inc[c][h]["scales"][:, edges],
+                        start=(c == 0 and t == 0),
+                        stop=(c == NODE_PASSES - 1 and t == CH_TILES - 1),
                     )
 
         def round_agg(i):
@@ -206,7 +207,7 @@ def tile_heterogeneoustemporalhypergraphnn_pa_kernel(
             )
 
         def project(i):
-            lin_banks[i] = main_psum.tile([P, N_CH], F32, tag="lin", name="lin_ps%d" % i)
+            lin_banks[i] = main_psum.tile([P, N_CH], F32, tag="bank", name="lin_ps%d" % i)
             nc.tensor.matmul_mx(
                 out=lin_banks[i][:],
                 lhsT=agg_codes[:, i, :].bitcast(FP8X4),
@@ -236,47 +237,28 @@ def tile_heterogeneoustemporalhypergraphnn_pa_kernel(
             bias_ps = setup_psum.tile([P, N_CH], F32)
             softmax_partial_max()
             softmax_exp()
-            regroup(nf[0])
             softmax_normalise()
-            for c in range(1, NODE_PASSES):
-                regroup(nf[c])
-                quantise(nf[c - 1])
             spread_bias()
         for i in range(EDGE_TILES):
             scale_bias(i)
 
-        with tc.psum_pool(name="main_psum", bufs=HALF) as main_psum:
-            regroup(inc[0][0])
-            quantise(nf[3])
-            for c in range(1, NODE_PASSES):
-                regroup(inc[0][c])
-                quantise(inc[0][c - 1])
-            quantise(inc[0][NODE_PASSES - 1])
-            for i in range(HALF):
-                aggregate(i)
-            regroup(inc[1][0])
-            for c in range(1, NODE_PASSES):
-                regroup(inc[1][c])
-                quantise(inc[1][c - 1])
-            quantise(inc[1][NODE_PASSES - 1])
-            for i in range(HALF // 2):
-                round_agg(i)
-                aggregate(HALF + i)
-            regroup(w1)
-            for i in range(HALF // 2):
-                quantise_agg(i)
-            quantise(w1)
-            for i in range(HALF // 2, HALF):
+        with tc.psum_pool(name="main_psum", bufs=EDGE_TILES) as main_psum:
+            for i in range(EDGE_TILES):
+                agg_banks.append(
+                    main_psum.tile([P, CH_TILES, P], F32, tag="bank", name="agg_ps%d" % i)
+                )
+            for c in range(NODE_PASSES):
+                regroup(nf[c])
+                quantise(nf[c])
+                if c == NODE_PASSES - 1:
+                    regroup(w1)
+                    quantise(w1)
+                for h in range(EDGE_CHUNKS):
+                    regroup(inc[c][h])
+                    quantise(inc[c][h])
+                    accumulate(c, h)
+            for i in range(EDGE_TILES):
                 round_agg(i)
                 quantise_agg(i)
-            for i in range(HALF):
                 project(i)
-            aggregate(HALF + 2)
-            aggregate(HALF + 3)
-            for i in range(HALF):
-                finish(i)
-                round_agg(HALF + i)
-                quantise_agg(HALF + i)
-                project(HALF + i)
-            for i in range(HALF, EDGE_TILES):
                 finish(i)

import concourse.mybir as mybir
from concourse.masks import make_identity

BF16 = mybir.dt.bfloat16
F32 = mybir.dt.float32
U32 = mybir.dt.uint32
U8 = mybir.dt.uint8
FP8X4 = mybir.dt.float8_e4m3fn_x4
ALU = mybir.AluOpType
ACT = mybir.ActivationFunctionType
AXIS = mybir.AxisListType

N_NODES, N_EDGES, N_CH = 2048, 1024, 512

P = 128
PACK = 4
K_PASS = P * PACK
WIDTH = 512
NODE_PASSES = N_NODES // K_PASS
CH_TILES = N_CH // P
EDGE_TILES = N_EDGES // P
EDGE_CHUNKS = N_EDGES // WIDTH
CHUNK_TILES = WIDTH // P
RUN = 4
SCALAR_COLS = 256

FLOPS = 2 * N_EDGES * N_NODES * N_CH + 2 * N_EDGES * N_CH * N_CH

assert CH_TILES == PACK and N_CH == WIDTH


def tile_heterogeneoustemporalhypergraphnn_pa_kernel(
    tc, node_features, incidence, W1, b1, edge_attention, out
):
    nc = tc.nc

    with tc.tile_pool(name="chunks", bufs=1) as chunk_pool, tc.tile_pool(
        name="agg", bufs=1
    ) as agg_pool, tc.tile_pool(name="small", bufs=1) as small_pool, tc.tile_pool(
        name="result", bufs=4
    ) as result_pool:
        def load_rows(name, width, rows_of_partition):
            rows = chunk_pool.tile([P, PACK, width], BF16, name=name + "_rows")
            nc.sync.dma_start(out=rows[:], in_=rows_of_partition)
            return rows

        def new_chunk(name, rows):
            return {
                "rows": rows,
                "grouped": chunk_pool.tile(
                    [P, WIDTH, PACK], BF16, align_bytes=64, name=name + "_grouped"
                ),
                "codes": chunk_pool.tile([P, WIDTH], U32, align_bytes=64, name=name + "_codes"),
                "scales": chunk_pool.tile([P, WIDTH], U8, align_bytes=64, name=name + "_scales"),
            }

        def regroup_columns(copy, chunk, cols):
            copy(
                out=chunk["grouped"][:, cols, :].rearrange("p (c i) j -> p c j i", i=RUN),
                in_=chunk["rows"][:, :, cols].rearrange("p j (c i) -> p c j i", i=RUN),
            )

        def regroup(chunk):
            regroup_columns(nc.scalar.copy, chunk, slice(0, SCALAR_COLS))
            regroup_columns(nc.vector.tensor_copy, chunk, slice(SCALAR_COLS, WIDTH))

        def quantise(chunk):
            nc.vector.quantize_mx(
                out=chunk["codes"][:].bitcast(FP8X4),
                scales=chunk["scales"][:],
                in_=chunk["grouped"][:].rearrange("p w j -> p (w j)"),
            )

        logit_rows = small_pool.tile([P, P], BF16)
        bias_rows = small_pool.tile([P, N_CH], BF16)
        ones_bf = small_pool.tile([P, P], BF16)
        ones_f32 = small_pool.tile([P, P], F32)
        ident_bf = small_pool.tile([P, P], BF16)
        table_warm = small_pool.tile([P, 1], F32)
        nc.gpsimd.memset(logit_rows[:], 0.0)
        nc.gpsimd.memset(bias_rows[:], 0.0)
        nc.vector.memset(table_warm[:], 0.0)
        nc.vector.memset(ones_bf[:], 1.0)
        nc.vector.memset(ones_f32[:], 1.0)
        make_identity(nc, ident_bf[:])
        nc.scalar.activation(out=table_warm[:], in_=table_warm[:], func=ACT.Exp)

        nc.sync.dma_start(
            out=logit_rows[0:EDGE_TILES, :],
            in_=edge_attention.rearrange("(i q) -> i q", q=P),
        )
        nf = []
        inc = []
        for c in range(NODE_PASSES):
            nodes = slice(c * K_PASS, (c + 1) * K_PASS)
            nf_rows = load_rows(
                "nf%d" % c, N_CH, node_features[nodes, :].rearrange("(p j) w -> p j w", j=PACK)
            )
            if c == 0:
                nc.sync.dma_start(out=bias_rows[0:1, :], in_=b1.rearrange("(o n) -> o n", o=1))
            if c == NODE_PASSES - 1:
                w1_rows = load_rows("w1", N_CH, W1.rearrange("(t p) n -> p t n", p=P))
            inc_rows = load_rows(
                "inc%d" % c, N_EDGES, incidence[nodes, :].rearrange("(p j) w -> p j w", j=PACK)
            )
            nf.append(new_chunk("nf%d" % c, nf_rows[:]))
            inc.append(
                [
                    new_chunk("inc%d_%d" % (c, h), inc_rows[:, :, h * WIDTH : (h + 1) * WIDTH])
                    for h in range(EDGE_CHUNKS)
                ]
            )
        w1 = new_chunk("w1", w1_rows[:])

        logit_col = small_pool.tile([P, EDGE_TILES], F32)
        part_max = small_pool.tile([P, 1], F32)
        part_max_bf = small_pool.tile([P, 1], BF16)
        all_max = small_pool.tile([P, 1], F32)
        shifted = small_pool.tile([P, EDGE_TILES], F32)
        exp_col = small_pool.tile([P, EDGE_TILES], F32)
        exp_sum = small_pool.tile([P, 1], F32)
        inv_sum = small_pool.tile([P, 1], F32)
        attn_col = small_pool.tile([P, EDGE_TILES], F32)

        def softmax_partial_max():
            nc.tensor.transpose(logit_ps[:], logit_rows[:], ident_bf[:])
            nc.vector.tensor_copy(out=logit_col[:], in_=logit_ps[:, 0:EDGE_TILES])
            nc.vector.tensor_reduce(out=part_max[:], in_=logit_col[:], axis=AXIS.X, op=ALU.max)
            nc.vector.tensor_copy(out=part_max_bf[:], in_=part_max[:])
            nc.tensor.matmul(
                out=max_ps[:],
                lhsT=part_max_bf[:, 0:1].to_broadcast([P, P]),
                rhs=ident_bf[:],
                start=True,
                stop=True,
            )

        def softmax_exp():
            nc.vector.tensor_reduce(out=all_max[:], in_=max_ps[:], axis=AXIS.X, op=ALU.max)
            nc.vector.tensor_scalar(
                out=shifted[:],
                in0=logit_col[:],
                scalar1=all_max[:, 0:1],
                scalar2=None,
                op0=ALU.subtract,
            )
            nc.scalar.activation(out=exp_col[:], in_=shifted[:], func=ACT.Exp)
            nc.tensor.matmul(out=sum_ps[:], lhsT=ones_f32[:], rhs=exp_col[:], start=True, stop=True)

        def softmax_normalise():
            nc.vector.tensor_reduce(out=exp_sum[:], in_=sum_ps[:], axis=AXIS.X, op=ALU.add)
            nc.vector.reciprocal(out=inv_sum[:], in_=exp_sum[:])
            nc.vector.tensor_scalar(
                out=attn_col[:],
                in0=exp_col[:],
                scalar1=inv_sum[:, 0:1],
                scalar2=None,
                op0=ALU.mult,
            )

        bias_all = small_pool.tile([P, N_CH], F32)
        bias_attn = small_pool.tile([P, EDGE_TILES, N_CH], F32)

        def spread_bias():
            nc.tensor.matmul(out=bias_ps[:], lhsT=ones_bf[:], rhs=bias_rows[:], start=True, stop=True)
            nc.scalar.copy(out=bias_all[:], in_=bias_ps[:])

        def scale_bias(i):
            nc.gpsimd.tensor_scalar(
                out=bias_attn[:, i, :],
                in0=bias_all[:],
                scalar1=attn_col[:, i : i + 1],
                scalar2=0.0,
                op0=ALU.mult,
                op1=ALU.add,
            )

        agg_grouped = agg_pool.tile([P, EDGE_TILES, P, PACK], BF16, align_bytes=64)
        agg_codes = agg_pool.tile([P, EDGE_TILES, P], U32, align_bytes=64)
        agg_scales = agg_pool.tile([P, EDGE_TILES, P], U8, align_bytes=64)
        agg_banks = []
        lin_banks = {}

        def accumulate(c, h):
            for k in range(CHUNK_TILES):
                edges = slice(k * P, (k + 1) * P)
                for t in range(CH_TILES):
                    channels = slice(t * P, (t + 1) * P)
                    nc.tensor.matmul_mx(
                        out=agg_banks[h * CHUNK_TILES + k][:, t, :],
                        lhsT=nf[c]["codes"][:, channels].bitcast(FP8X4),
                        lhsT_scale=nf[c]["scales"][:, channels],
                        rhs=inc[c][h]["codes"][:, edges].bitcast(FP8X4),
                        rhs_scale=inc[c][h]["scales"][:, edges],
                        start=(c == 0 and t == 0),
                        stop=(c == NODE_PASSES - 1 and t == CH_TILES - 1),
                    )

        def round_agg(i):
            nc.scalar.copy(out=agg_grouped[:, i], in_=agg_banks[i][:].rearrange("p t e -> p e t"))

        def quantise_agg(i):
            nc.vector.quantize_mx(
                out=agg_codes[:, i, :].bitcast(FP8X4),
                scales=agg_scales[:, i, :],
                in_=agg_grouped[:, i].rearrange("p e t -> p (e t)"),
            )

        def project(i):
            lin_banks[i] = main_psum.tile([P, N_CH], F32, tag="bank", name="lin_ps%d" % i)
            nc.tensor.matmul_mx(
                out=lin_banks[i][:],
                lhsT=agg_codes[:, i, :].bitcast(FP8X4),
                lhsT_scale=agg_scales[:, i, :],
                rhs=w1["codes"][:].bitcast(FP8X4),
                rhs_scale=w1["scales"][:],
                start=True,
                stop=True,
            )

        def finish(i):
            result = result_pool.tile([P, N_CH], F32)
            nc.vector.scalar_tensor_tensor(
                out=result[:],
                in0=lin_banks[i][:],
                scalar=attn_col[:, i : i + 1],
                in1=bias_attn[:, i, :],
                op0=ALU.mult,
                op1=ALU.add,
            )
            nc.sync.dma_start(out=out[i * P : (i + 1) * P, :], in_=result[:])

        with tc.psum_pool(name="setup_psum", bufs=1) as setup_psum:
            logit_ps = setup_psum.tile([P, P], BF16)
            max_ps = setup_psum.tile([P, P], F32)
            sum_ps = setup_psum.tile([P, EDGE_TILES], F32)
            bias_ps = setup_psum.tile([P, N_CH], F32)
            softmax_partial_max()
            softmax_exp()
            softmax_normalise()
            spread_bias()
        for i in range(EDGE_TILES):
            scale_bias(i)

        with tc.psum_pool(name="main_psum", bufs=EDGE_TILES) as main_psum:
            for i in range(EDGE_TILES):
                agg_banks.append(
                    main_psum.tile([P, CH_TILES, P], F32, tag="bank", name="agg_ps%d" % i)
                )
            for c in range(NODE_PASSES):
                regroup(nf[c])
                quantise(nf[c])
                if c == NODE_PASSES - 1:
                    regroup(w1)
                    quantise(w1)
                for h in range(EDGE_CHUNKS):
                    regroup(inc[c][h])
                    quantise(inc[c][h])
                    accumulate(c, h)
            for i in range(EDGE_TILES):
                round_agg(i)
                quantise_agg(i)
                project(i)
                finish(i)
